import numpy as np
import ml_dtypes

BF16 = ml_dtypes.bfloat16


def bf(x):
    return np.asarray(x, np.float32).astype(BF16)


def f32(x):
    return np.asarray(x, np.float32)


def f64(x):
    return np.asarray(x).astype(np.float64)


def striped(idx):
    return np.tile(idx.reshape(-1, 16).T, (8, 1))


C, E, T, S, N = 128, 128, 384, 1024, 512


def sigmoid(v):
    return 1.0 / (1.0 + np.exp(-v))


def setup_inputs():
    return {"base": f32(np.random.standard_normal((C, S))), "emb": bf(np.random.standard_normal((E, N))), "hid": bf(np.random.standard_normal((C, N))), "w_ih": bf(np.random.standard_normal((E, T)) / np.sqrt(E)), "w_hh": bf(np.random.standard_normal((C, T)) / np.sqrt(C)), "b_ih": f32(0.3 * np.random.standard_normal((T, 1))), "b_hh": f32(0.3 * np.random.standard_normal((T, 1))), "offs": striped(np.random.permutation(S)[:N])}


def reference(base, emb, hid, w_ih, w_hh, b_ih, b_hh, offs):
    idx = offs[:16].T.reshape(-1)
    gi = f64(w_ih).T @ f64(emb) + f64(b_ih)
    gh = f64(w_hh).T @ f64(hid) + f64(b_hh)
    r = sigmoid(gi[:C] + gh[:C])
    z = sigmoid(gi[C:T - C] + gh[C:T - C])
    cand = np.tanh(gi[T - C:] + r * gh[T - C:])
    out = f64(base).copy()
    out[:, idx] = (1.0 - z) * cand + z * f64(hid)
    return out

@@ -1,0 +1,73 @@
+import concourse.mybir as mybir
+
+P = 128
+N = 512
+S = 1024
+GATES = 3
+
+FLOPS = 2 * 2 * P * GATES * P * N
+
+BF16, F32, U16 = mybir.dt.bfloat16, mybir.dt.float32, mybir.dt.uint16
+ADD, MULT = mybir.AluOpType.add, mybir.AluOpType.mult
+SIGMOID, TANH = mybir.ActivationFunctionType.Sigmoid, mybir.ActivationFunctionType.Tanh
+
+
+def tile_decoder_attn_kernel(tc, base, emb, hid, w_ih, w_hh, b_ih, b_hh, offs, out):
+    nc = tc.nc
+    with (
+        tc.tile_pool(name="held", bufs=1) as held,
+        tc.psum_pool(name="psum", bufs=1) as psum,
+    ):
+        offsets = held.tile([P, N // 16], U16, name="offsets")
+        nc.sync.dma_start(offsets[:], offs)
+        w_ih_sb = held.tile([P, GATES * P], BF16, name="w_ih_sb")
+        nc.sync.dma_start(w_ih_sb[:], w_ih)
+        emb_sb = held.tile([P, N], BF16, name="emb_sb")
+        nc.sync.dma_start(emb_sb[:], emb)
+        w_hh_sb = held.tile([P, GATES * P], BF16, name="w_hh_sb")
+        nc.scalar.dma_start(w_hh_sb[:], w_hh)
+        hid_sb = held.tile([P, N], BF16, name="hid_sb")
+        nc.scalar.dma_start(hid_sb[:], hid)
+        b_ih_sb = held.tile([P, GATES], F32, name="b_ih_sb")
+        b_hh_sb = held.tile([P, GATES], F32, name="b_hh_sb")
+        with nc.allow_non_contiguous_dma(reason="384 bias values, one to a partition and gate"):
+            nc.gpsimd.dma_start(b_ih_sb[:], b_ih.rearrange("(g c) o -> c (g o)", g=GATES))
+            nc.gpsimd.dma_start(b_hh_sb[:], b_hh.rearrange("(g c) o -> c (g o)", g=GATES))
+        window = held.tile([P, S], F32, name="window")
+        nc.sync.dma_start(window[:], base)
+
+        b_sum = held.tile([P, 2], F32, name="b_sum")
+        nc.vector.tensor_tensor(b_sum[:], b_ih_sb[:, 0:2], b_hh_sb[:, 0:2], ADD)
+        b_z_neg = held.tile([P, 1], F32, name="b_z_neg")
+        nc.vector.tensor_scalar_mul(b_z_neg[:], b_sum[:, 1:2], -1.0)
+
+        ps_r = psum.tile([P, N], F32, name="ps_r")
+        nc.tensor.matmul(ps_r[:], w_ih_sb[:, 0:P], emb_sb[:], start=True, stop=False)
+        nc.tensor.matmul(ps_r[:], w_hh_sb[:, 0:P], hid_sb[:], start=False, stop=True)
+        ps_gh_n = psum.tile([P, N], F32, name="ps_gh_n")
+        nc.tensor.matmul(ps_gh_n[:], w_hh_sb[:, 2 * P : 3 * P], hid_sb[:], start=True, stop=True)
+        ps_gi_n = psum.tile([P, N], F32, name="ps_gi_n")
+        nc.tensor.matmul(ps_gi_n[:], w_ih_sb[:, 2 * P : 3 * P], emb_sb[:], start=True, stop=True)
+        ps_z = psum.tile([P, N], F32, name="ps_z")
+        nc.tensor.matmul(ps_z[:], w_ih_sb[:, P : 2 * P], emb_sb[:], start=True, stop=False)
+        nc.tensor.matmul(ps_z[:], w_hh_sb[:, P : 2 * P], hid_sb[:], start=False, stop=True)
+
+        r = held.tile([P, N], F32, name="r")
+        nc.scalar.activation(r[:], ps_r[:], SIGMOID, bias=b_sum[:, 0:1], scale=1.0)
+        r_gh = held.tile([P, N], F32, name="r_gh")
+        nc.vector.scalar_tensor_tensor(r_gh[:], ps_gh_n[:], b_hh_sb[:, 2:3], r[:], ADD, MULT)
+        pre = held.tile([P, N], F32, name="pre")
+        nc.vector.tensor_tensor(pre[:], r_gh[:], ps_gi_n[:], ADD)
+        z = held.tile([P, N], F32, name="z")
+        nc.scalar.activation(z[:], ps_z[:], SIGMOID, bias=b_sum[:, 1:2], scale=1.0)
+        z_rest = held.tile([P, N], F32, name="z_rest")
+        nc.scalar.activation(z_rest[:], ps_z[:], SIGMOID, bias=b_z_neg[:], scale=-1.0)
+        cand = held.tile([P, N], F32, name="cand")
+        nc.scalar.activation(cand[:], pre[:], TANH, bias=b_ih_sb[:, 2:3], scale=1.0)
+        kept = held.tile([P, N], F32, name="kept")
+        nc.vector.tensor_tensor(kept[:], z[:], hid_sb[:], MULT)
+        fresh = held.tile([P, N], F32, name="fresh")
+        nc.vector.tensor_tensor(fresh[:], z_rest[:], cand[:], MULT)
+
+        nc.vector.tensor_tensor(window[:].indirect(offsets[:]), fresh[:], kept[:], ADD)
+        nc.sync.dma_start(out, window[:])

@@ -18,28 +18,28 @@ def tile_decoder_attn_kernel(tc, base, emb, hid, w_ih, w_hh, b_ih, b_hh, offs, o
         tc.tile_pool(name="held", bufs=1) as held,
         tc.psum_pool(name="psum", bufs=1) as psum,
     ):
-        offsets = held.tile([P, N // 16], U16, name="offsets")
-        nc.sync.dma_start(offsets[:], offs)
         w_ih_sb = held.tile([P, GATES * P], BF16, name="w_ih_sb")
         nc.sync.dma_start(w_ih_sb[:], w_ih)
-        emb_sb = held.tile([P, N], BF16, name="emb_sb")
-        nc.sync.dma_start(emb_sb[:], emb)
         w_hh_sb = held.tile([P, GATES * P], BF16, name="w_hh_sb")
         nc.scalar.dma_start(w_hh_sb[:], w_hh)
+        emb_sb = held.tile([P, N], BF16, name="emb_sb")
+        nc.sync.dma_start(emb_sb[:], emb)
         hid_sb = held.tile([P, N], BF16, name="hid_sb")
         nc.scalar.dma_start(hid_sb[:], hid)
         b_ih_sb = held.tile([P, GATES], F32, name="b_ih_sb")
         b_hh_sb = held.tile([P, GATES], F32, name="b_hh_sb")
         with nc.allow_non_contiguous_dma(reason="384 bias values, one to a partition and gate"):
-            nc.gpsimd.dma_start(b_ih_sb[:], b_ih.rearrange("(g c) o -> c (g o)", g=GATES))
-            nc.gpsimd.dma_start(b_hh_sb[:], b_hh.rearrange("(g c) o -> c (g o)", g=GATES))
+            nc.sync.dma_start(b_ih_sb[:], b_ih.rearrange("(g c) o -> c (g o)", g=GATES))
+            nc.scalar.dma_start(b_hh_sb[:], b_hh.rearrange("(g c) o -> c (g o)", g=GATES))
+        offsets = held.tile([P, N // 16], U16, name="offsets")
+        nc.sync.dma_start(offsets[:], offs)
         window = held.tile([P, S], F32, name="window")
         nc.sync.dma_start(window[:], base)
 
         b_sum = held.tile([P, 2], F32, name="b_sum")
         nc.vector.tensor_tensor(b_sum[:], b_ih_sb[:, 0:2], b_hh_sb[:, 0:2], ADD)
-        b_z_neg = held.tile([P, 1], F32, name="b_z_neg")
-        nc.vector.tensor_scalar_mul(b_z_neg[:], b_sum[:, 1:2], -1.0)
+        b_in_neg = held.tile([P, 1], F32, name="b_in_neg")
+        nc.vector.tensor_scalar_mul(b_in_neg[:], b_ih_sb[:, 2:3], -1.0)
 
         ps_r = psum.tile([P, N], F32, name="ps_r")
         nc.tensor.matmul(ps_r[:], w_ih_sb[:, 0:P], emb_sb[:], start=True, stop=False)
@@ -60,14 +60,12 @@ def tile_decoder_attn_kernel(tc, base, emb, hid, w_ih, w_hh, b_ih, b_hh, offs, o
         nc.vector.tensor_tensor(pre[:], r_gh[:], ps_gi_n[:], ADD)
         z = held.tile([P, N], F32, name="z")
         nc.scalar.activation(z[:], ps_z[:], SIGMOID, bias=b_sum[:, 1:2], scale=1.0)
-        z_rest = held.tile([P, N], F32, name="z_rest")
-        nc.scalar.activation(z_rest[:], ps_z[:], SIGMOID, bias=b_z_neg[:], scale=-1.0)
-        cand = held.tile([P, N], F32, name="cand")
-        nc.scalar.activation(cand[:], pre[:], TANH, bias=b_ih_sb[:, 2:3], scale=1.0)
         kept = held.tile([P, N], F32, name="kept")
         nc.vector.tensor_tensor(kept[:], z[:], hid_sb[:], MULT)
+        cand_neg = held.tile([P, N], F32, name="cand_neg")
+        nc.scalar.activation(cand_neg[:], pre[:], TANH, bias=b_in_neg[:], scale=-1.0)
         fresh = held.tile([P, N], F32, name="fresh")
-        nc.vector.tensor_tensor(fresh[:], z_rest[:], cand[:], MULT)
+        nc.vector.scalar_tensor_tensor(fresh[:], z[:], -1.0, cand_neg[:], ADD, MULT)
 
         nc.vector.tensor_tensor(window[:].indirect(offsets[:]), fresh[:], kept[:], ADD)
         nc.sync.dma_start(out, window[:])

@@ -36,6 +36,11 @@ def tile_decoder_attn_kernel(tc, base, emb, hid, w_ih, w_hh, b_ih, b_hh, offs, o
         window = held.tile([P, S], F32, name="window")
         nc.sync.dma_start(window[:], base)
 
+        tiny = held.tile([P, 1], F32, name="tiny")
+        nc.gpsimd.memset(tiny[:], 0.0)
+        tiny_out = held.tile([P, 1], F32, name="tiny_out")
+        nc.scalar.activation(tiny_out[:], tiny[:], SIGMOID)
+
         b_sum = held.tile([P, 2], F32, name="b_sum")
         nc.vector.tensor_tensor(b_sum[:], b_ih_sb[:, 0:2], b_hh_sb[:, 0:2], ADD)
         b_in_neg = held.tile([P, 1], F32, name="b_in_neg")

@@ -5,6 +5,8 @@ N = 512
 S = 1024
 GATES = 3
 
+WARM_MATMULS = 4
+
 FLOPS = 2 * 2 * P * GATES * P * N
 
 BF16, F32, U16 = mybir.dt.bfloat16, mybir.dt.float32, mybir.dt.uint16
@@ -40,6 +42,12 @@ def tile_decoder_attn_kernel(tc, base, emb, hid, w_ih, w_hh, b_ih, b_hh, offs, o
         nc.gpsimd.memset(tiny[:], 0.0)
         tiny_out = held.tile([P, 1], F32, name="tiny_out")
         nc.scalar.activation(tiny_out[:], tiny[:], SIGMOID)
+
+        zeros = held.tile([P, N], BF16, name="zeros")
+        nc.vector.memset(zeros[:], 0.0)
+        ps_idle = psum.tile([P, N], F32, name="ps_idle")
+        for i in range(WARM_MATMULS):
+            nc.tensor.matmul(ps_idle[:], zeros[:, 0:P], zeros[:], start=True, stop=True)
 
         b_sum = held.tile([P, 2], F32, name="b_sum")
         nc.vector.tensor_tensor(b_sum[:], b_ih_sb[:, 0:2], b_hh_sb[:, 0:2], ADD)

@@ -4,14 +4,21 @@ P = 128
 N = 512
 S = 1024
 GATES = 3
+RESET, UPDATE, CAND = slice(0, P), slice(P, 2 * P), slice(2 * P, 3 * P)
+CHUNKS = 2
+W = N // CHUNKS
 
-WARM_MATMULS = 4
+WARM_MATMULS = 12
 
 FLOPS = 2 * 2 * P * GATES * P * N
 
 BF16, F32, U16 = mybir.dt.bfloat16, mybir.dt.float32, mybir.dt.uint16
 ADD, MULT = mybir.AluOpType.add, mybir.AluOpType.mult
 SIGMOID, TANH = mybir.ActivationFunctionType.Sigmoid, mybir.ActivationFunctionType.Tanh
+
+
+def cols(c):
+    return slice(c * W, (c + 1) * W)
 
 
 def tile_decoder_attn_kernel(tc, base, emb, hid, w_ih, w_hh, b_ih, b_hh, offs, out):
@@ -43,42 +50,51 @@ def tile_decoder_attn_kernel(tc, base, emb, hid, w_ih, w_hh, b_ih, b_hh, offs, o
         tiny_out = held.tile([P, 1], F32, name="tiny_out")
         nc.scalar.activation(tiny_out[:], tiny[:], SIGMOID)
 
-        zeros = held.tile([P, N], BF16, name="zeros")
+        zeros = held.tile([P, P], BF16, name="zeros")
         nc.vector.memset(zeros[:], 0.0)
-        ps_idle = psum.tile([P, N], F32, name="ps_idle")
+        ps_idle = psum.tile([P, P], F32, name="ps_idle")
         for i in range(WARM_MATMULS):
-            nc.tensor.matmul(ps_idle[:], zeros[:, 0:P], zeros[:], start=True, stop=True)
+            nc.tensor.matmul(ps_idle[:], zeros[:], zeros[:], start=True, stop=True)
 
         b_sum = held.tile([P, 2], F32, name="b_sum")
         nc.vector.tensor_tensor(b_sum[:], b_ih_sb[:, 0:2], b_hh_sb[:, 0:2], ADD)
         b_in_neg = held.tile([P, 1], F32, name="b_in_neg")
         nc.vector.tensor_scalar_mul(b_in_neg[:], b_ih_sb[:, 2:3], -1.0)
 
-        ps_r = psum.tile([P, N], F32, name="ps_r")
-        nc.tensor.matmul(ps_r[:], w_ih_sb[:, 0:P], emb_sb[:], start=True, stop=False)
-        nc.tensor.matmul(ps_r[:], w_hh_sb[:, 0:P], hid_sb[:], start=False, stop=True)
-        ps_gh_n = psum.tile([P, N], F32, name="ps_gh_n")
-        nc.tensor.matmul(ps_gh_n[:], w_hh_sb[:, 2 * P : 3 * P], hid_sb[:], start=True, stop=True)
-        ps_gi_n = psum.tile([P, N], F32, name="ps_gi_n")
-        nc.tensor.matmul(ps_gi_n[:], w_ih_sb[:, 2 * P : 3 * P], emb_sb[:], start=True, stop=True)
+        ps_r = [psum.tile([P, W], F32, name=f"ps_r{c}") for c in range(CHUNKS)]
+        ps_gi_n = [psum.tile([P, W], F32, name=f"ps_gi_n{c}") for c in range(CHUNKS)]
+        ps_gh_n = [psum.tile([P, W], F32, name=f"ps_gh_n{c}") for c in range(CHUNKS)]
         ps_z = psum.tile([P, N], F32, name="ps_z")
-        nc.tensor.matmul(ps_z[:], w_ih_sb[:, P : 2 * P], emb_sb[:], start=True, stop=False)
-        nc.tensor.matmul(ps_z[:], w_hh_sb[:, P : 2 * P], hid_sb[:], start=False, stop=True)
+        for c in range(CHUNKS):
+            nc.tensor.matmul(ps_r[c][:], w_ih_sb[:, RESET], emb_sb[:, cols(c)], start=True, stop=False)
+            nc.tensor.matmul(ps_r[c][:], w_hh_sb[:, RESET], hid_sb[:, cols(c)], start=False, stop=True)
+        for c in range(CHUNKS):
+            nc.tensor.matmul(ps_gh_n[c][:], w_hh_sb[:, CAND], hid_sb[:, cols(c)], start=True, stop=True)
+        nc.tensor.matmul(ps_z[:], w_ih_sb[:, UPDATE], emb_sb[:], start=True, stop=False)
+        nc.tensor.matmul(ps_z[:], w_hh_sb[:, UPDATE], hid_sb[:], start=False, stop=True)
+        for c in range(CHUNKS):
+            nc.tensor.matmul(ps_gi_n[c][:], w_ih_sb[:, CAND], emb_sb[:, cols(c)], start=True, stop=True)
 
         r = held.tile([P, N], F32, name="r")
-        nc.scalar.activation(r[:], ps_r[:], SIGMOID, bias=b_sum[:, 0:1], scale=1.0)
         r_gh = held.tile([P, N], F32, name="r_gh")
-        nc.vector.scalar_tensor_tensor(r_gh[:], ps_gh_n[:], b_hh_sb[:, 2:3], r[:], ADD, MULT)
         pre = held.tile([P, N], F32, name="pre")
-        nc.vector.tensor_tensor(pre[:], r_gh[:], ps_gi_n[:], ADD)
         z = held.tile([P, N], F32, name="z")
-        nc.scalar.activation(z[:], ps_z[:], SIGMOID, bias=b_sum[:, 1:2], scale=1.0)
         kept = held.tile([P, N], F32, name="kept")
-        nc.vector.tensor_tensor(kept[:], z[:], hid_sb[:], MULT)
         cand_neg = held.tile([P, N], F32, name="cand_neg")
-        nc.scalar.activation(cand_neg[:], pre[:], TANH, bias=b_in_neg[:], scale=-1.0)
         fresh = held.tile([P, N], F32, name="fresh")
-        nc.vector.scalar_tensor_tensor(fresh[:], z[:], -1.0, cand_neg[:], ADD, MULT)
+        for c in range(CHUNKS):
+            nc.scalar.activation(r[:, cols(c)], ps_r[c][:], SIGMOID, bias=b_sum[:, 0:1], scale=1.0)
+            nc.vector.scalar_tensor_tensor(
+                r_gh[:, cols(c)], ps_gh_n[c][:], b_hh_sb[:, 2:3], r[:, cols(c)], ADD, MULT
+            )
+            nc.vector.tensor_tensor(pre[:, cols(c)], r_gh[:, cols(c)], ps_gi_n[c][:], ADD)
+        nc.scalar.activation(z[:], ps_z[:], SIGMOID, bias=b_sum[:, 1:2], scale=1.0)
+        nc.vector.tensor_tensor(kept[:], z[:], hid_sb[:], MULT)
+        for c in range(CHUNKS):
+            nc.scalar.activation(cand_neg[:, cols(c)], pre[:, cols(c)], TANH, bias=b_in_neg[:], scale=-1.0)
+            nc.vector.scalar_tensor_tensor(
+                fresh[:, cols(c)], z[:, cols(c)], -1.0, cand_neg[:, cols(c)], ADD, MULT
+            )
 
         nc.vector.tensor_tensor(window[:].indirect(offsets[:]), fresh[:], kept[:], ADD)
         nc.sync.dma_start(out, window[:])

@@ -43,7 +43,7 @@ def tile_decoder_attn_kernel(tc, base, emb, hid, w_ih, w_hh, b_ih, b_hh, offs, o
         offsets = held.tile([P, N // 16], U16, name="offsets")
         nc.sync.dma_start(offsets[:], offs)
         window = held.tile([P, S], F32, name="window")
-        nc.sync.dma_start(window[:], base)
+        nc.gpsimd.dma_start(window[:], base)
 
         tiny = held.tile([P, 1], F32, name="tiny")
         nc.gpsimd.memset(tiny[:], 0.0)

@@ -5,7 +5,9 @@ N = 512
 S = 1024
 GATES = 3
 RESET, UPDATE, CAND = slice(0, P), slice(P, 2 * P), slice(2 * P, 3 * P)
-CHUNKS = 2
+BANKS = 2
+WB = N // BANKS
+CHUNKS = 4
 W = N // CHUNKS
 
 WARM_MATMULS = 12
@@ -19,6 +21,15 @@ SIGMOID, TANH = mybir.ActivationFunctionType.Sigmoid, mybir.ActivationFunctionTy
 
 def cols(c):
     return slice(c * W, (c + 1) * W)
+
+
+def bank_cols(b):
+    return slice(b * WB, (b + 1) * WB)
+
+
+def in_bank(tiles, c):
+    b, start = divmod(c * W, WB)
+    return tiles[b][:, start : start + W]
 
 
 def tile_decoder_attn_kernel(tc, base, emb, hid, w_ih, w_hh, b_ih, b_hh, offs, out):
@@ -43,7 +54,7 @@ def tile_decoder_attn_kernel(tc, base, emb, hid, w_ih, w_hh, b_ih, b_hh, offs, o
         offsets = held.tile([P, N // 16], U16, name="offsets")
         nc.sync.dma_start(offsets[:], offs)
         window = held.tile([P, S], F32, name="window")
-        nc.gpsimd.dma_start(window[:], base)
+        nc.sync.dma_start(window[:], base)
 
         tiny = held.tile([P, 1], F32, name="tiny")
         nc.gpsimd.memset(tiny[:], 0.0)
@@ -61,19 +72,19 @@ def tile_decoder_attn_kernel(tc, base, emb, hid, w_ih, w_hh, b_ih, b_hh, offs, o
         b_in_neg = held.tile([P, 1], F32, name="b_in_neg")
         nc.vector.tensor_scalar_mul(b_in_neg[:], b_ih_sb[:, 2:3], -1.0)
 
-        ps_r = [psum.tile([P, W], F32, name=f"ps_r{c}") for c in range(CHUNKS)]
-        ps_gi_n = [psum.tile([P, W], F32, name=f"ps_gi_n{c}") for c in range(CHUNKS)]
-        ps_gh_n = [psum.tile([P, W], F32, name=f"ps_gh_n{c}") for c in range(CHUNKS)]
+        ps_r = [psum.tile([P, WB], F32, name=f"ps_r{b}") for b in range(BANKS)]
+        ps_gi_n = [psum.tile([P, WB], F32, name=f"ps_gi_n{b}") for b in range(BANKS)]
+        ps_gh_n = [psum.tile([P, WB], F32, name=f"ps_gh_n{b}") for b in range(BANKS)]
         ps_z = psum.tile([P, N], F32, name="ps_z")
-        for c in range(CHUNKS):
-            nc.tensor.matmul(ps_r[c][:], w_ih_sb[:, RESET], emb_sb[:, cols(c)], start=True, stop=False)
-            nc.tensor.matmul(ps_r[c][:], w_hh_sb[:, RESET], hid_sb[:, cols(c)], start=False, stop=True)
-        for c in range(CHUNKS):
-            nc.tensor.matmul(ps_gh_n[c][:], w_hh_sb[:, CAND], hid_sb[:, cols(c)], start=True, stop=True)
+        for b in range(BANKS):
+            nc.tensor.matmul(ps_r[b][:], w_ih_sb[:, RESET], emb_sb[:, bank_cols(b)], start=True, stop=False)
+            nc.tensor.matmul(ps_r[b][:], w_hh_sb[:, RESET], hid_sb[:, bank_cols(b)], start=False, stop=True)
+        for b in range(BANKS):
+            nc.tensor.matmul(ps_gh_n[b][:], w_hh_sb[:, CAND], hid_sb[:, bank_cols(b)], start=True, stop=True)
         nc.tensor.matmul(ps_z[:], w_ih_sb[:, UPDATE], emb_sb[:], start=True, stop=False)
         nc.tensor.matmul(ps_z[:], w_hh_sb[:, UPDATE], hid_sb[:], start=False, stop=True)
-        for c in range(CHUNKS):
-            nc.tensor.matmul(ps_gi_n[c][:], w_ih_sb[:, CAND], emb_sb[:, cols(c)], start=True, stop=True)
+        for b in range(BANKS):
+            nc.tensor.matmul(ps_gi_n[b][:], w_ih_sb[:, CAND], emb_sb[:, bank_cols(b)], start=True, stop=True)
 
         r = held.tile([P, N], F32, name="r")
         r_gh = held.tile([P, N], F32, name="r_gh")
@@ -83,11 +94,11 @@ def tile_decoder_attn_kernel(tc, base, emb, hid, w_ih, w_hh, b_ih, b_hh, offs, o
         cand_neg = held.tile([P, N], F32, name="cand_neg")
         fresh = held.tile([P, N], F32, name="fresh")
         for c in range(CHUNKS):
-            nc.scalar.activation(r[:, cols(c)], ps_r[c][:], SIGMOID, bias=b_sum[:, 0:1], scale=1.0)
+            nc.scalar.activation(r[:, cols(c)], in_bank(ps_r, c), SIGMOID, bias=b_sum[:, 0:1], scale=1.0)
             nc.vector.scalar_tensor_tensor(
-                r_gh[:, cols(c)], ps_gh_n[c][:], b_hh_sb[:, 2:3], r[:, cols(c)], ADD, MULT
+                r_gh[:, cols(c)], in_bank(ps_gh_n, c), b_hh_sb[:, 2:3], r[:, cols(c)], ADD, MULT
             )
-            nc.vector.tensor_tensor(pre[:, cols(c)], r_gh[:, cols(c)], ps_gi_n[c][:], ADD)
+            nc.vector.tensor_tensor(pre[:, cols(c)], r_gh[:, cols(c)], in_bank(ps_gi_n, c), ADD)
         nc.scalar.activation(z[:], ps_z[:], SIGMOID, bias=b_sum[:, 1:2], scale=1.0)
         nc.vector.tensor_tensor(kept[:], z[:], hid_sb[:], MULT)
         for c in range(CHUNKS):

@@ -63,9 +63,9 @@ def tile_decoder_attn_kernel(tc, base, emb, hid, w_ih, w_hh, b_ih, b_hh, offs, o
 
         zeros = held.tile([P, P], BF16, name="zeros")
         nc.vector.memset(zeros[:], 0.0)
-        ps_idle = psum.tile([P, P], F32, name="ps_idle")
+        ps_z = [psum.tile([P, WB], F32, name=f"ps_z{b}") for b in range(BANKS)]
         for i in range(WARM_MATMULS):
-            nc.tensor.matmul(ps_idle[:], zeros[:], zeros[:], start=True, stop=True)
+            nc.tensor.matmul(ps_z[BANKS - 1][:, 0:P], zeros[:], zeros[:], start=True, stop=True)
 
         b_sum = held.tile([P, 2], F32, name="b_sum")
         nc.vector.tensor_tensor(b_sum[:], b_ih_sb[:, 0:2], b_hh_sb[:, 0:2], ADD)
@@ -75,14 +75,14 @@ def tile_decoder_attn_kernel(tc, base, emb, hid, w_ih, w_hh, b_ih, b_hh, offs, o
         ps_r = [psum.tile([P, WB], F32, name=f"ps_r{b}") for b in range(BANKS)]
         ps_gi_n = [psum.tile([P, WB], F32, name=f"ps_gi_n{b}") for b in range(BANKS)]
         ps_gh_n = [psum.tile([P, WB], F32, name=f"ps_gh_n{b}") for b in range(BANKS)]
-        ps_z = psum.tile([P, N], F32, name="ps_z")
         for b in range(BANKS):
             nc.tensor.matmul(ps_r[b][:], w_ih_sb[:, RESET], emb_sb[:, bank_cols(b)], start=True, stop=False)
             nc.tensor.matmul(ps_r[b][:], w_hh_sb[:, RESET], hid_sb[:, bank_cols(b)], start=False, stop=True)
         for b in range(BANKS):
             nc.tensor.matmul(ps_gh_n[b][:], w_hh_sb[:, CAND], hid_sb[:, bank_cols(b)], start=True, stop=True)
-        nc.tensor.matmul(ps_z[:], w_ih_sb[:, UPDATE], emb_sb[:], start=True, stop=False)
-        nc.tensor.matmul(ps_z[:], w_hh_sb[:, UPDATE], hid_sb[:], start=False, stop=True)
+        for b in range(BANKS):
+            nc.tensor.matmul(ps_z[b][:], w_ih_sb[:, UPDATE], emb_sb[:, bank_cols(b)], start=True, stop=False)
+            nc.tensor.matmul(ps_z[b][:], w_hh_sb[:, UPDATE], hid_sb[:, bank_cols(b)], start=False, stop=True)
         for b in range(BANKS):
             nc.tensor.matmul(ps_gi_n[b][:], w_ih_sb[:, CAND], emb_sb[:, bank_cols(b)], start=True, stop=True)
 
@@ -99,8 +99,10 @@ def tile_decoder_attn_kernel(tc, base, emb, hid, w_ih, w_hh, b_ih, b_hh, offs, o
                 r_gh[:, cols(c)], in_bank(ps_gh_n, c), b_hh_sb[:, 2:3], r[:, cols(c)], ADD, MULT
             )
             nc.vector.tensor_tensor(pre[:, cols(c)], r_gh[:, cols(c)], in_bank(ps_gi_n, c), ADD)
-        nc.scalar.activation(z[:], ps_z[:], SIGMOID, bias=b_sum[:, 1:2], scale=1.0)
-        nc.vector.tensor_tensor(kept[:], z[:], hid_sb[:], MULT)
+        for b in range(BANKS):
+            x = bank_cols(b)
+            nc.scalar.activation(z[:, x], ps_z[b][:], SIGMOID, bias=b_sum[:, 1:2], scale=1.0)
+            nc.gpsimd.tensor_tensor(kept[:, x], z[:, x], hid_sb[:, x], MULT)
         for c in range(CHUNKS):
             nc.scalar.activation(cand_neg[:, cols(c)], pre[:, cols(c)], TANH, bias=b_in_neg[:], scale=-1.0)
             nc.vector.scalar_tensor_tensor(

@@ -83,7 +83,6 @@ def tile_decoder_attn_kernel(tc, base, emb, hid, w_ih, w_hh, b_ih, b_hh, offs, o
         for b in range(BANKS):
             nc.tensor.matmul(ps_z[b][:], w_ih_sb[:, UPDATE], emb_sb[:, bank_cols(b)], start=True, stop=False)
             nc.tensor.matmul(ps_z[b][:], w_hh_sb[:, UPDATE], hid_sb[:, bank_cols(b)], start=False, stop=True)
-        for b in range(BANKS):
             nc.tensor.matmul(ps_gi_n[b][:], w_ih_sb[:, CAND], emb_sb[:, bank_cols(b)], start=True, stop=True)
 
         r = held.tile([P, N], F32, name="r")
@@ -102,7 +101,7 @@ def tile_decoder_attn_kernel(tc, base, emb, hid, w_ih, w_hh, b_ih, b_hh, offs, o
         for b in range(BANKS):
             x = bank_cols(b)
             nc.scalar.activation(z[:, x], ps_z[b][:], SIGMOID, bias=b_sum[:, 1:2], scale=1.0)
-            nc.gpsimd.tensor_tensor(kept[:, x], z[:, x], hid_sb[:, x], MULT)
+            nc.vector.tensor_tensor(kept[:, x], z[:, x], hid_sb[:, x], MULT)
         for c in range(CHUNKS):
             nc.scalar.activation(cand_neg[:, cols(c)], pre[:, cols(c)], TANH, bias=b_in_neg[:], scale=-1.0)
             nc.vector.scalar_tensor_tensor(

@@ -54,7 +54,7 @@ def tile_decoder_attn_kernel(tc, base, emb, hid, w_ih, w_hh, b_ih, b_hh, offs, o
         offsets = held.tile([P, N // 16], U16, name="offsets")
         nc.sync.dma_start(offsets[:], offs)
         window = held.tile([P, S], F32, name="window")
-        nc.sync.dma_start(window[:], base)
+        nc.gpsimd.dma_start(window[:], base)
 
         tiny = held.tile([P, 1], F32, name="tiny")
         nc.gpsimd.memset(tiny[:], 0.0)

@@ -4,6 +4,7 @@ P = 128
 N = 512
 S = 1024
 GATES = 3
+BLK = 32
 RESET, UPDATE, CAND = slice(0, P), slice(P, 2 * P), slice(2 * P, 3 * P)
 BANKS = 2
 WB = N // BANKS
@@ -46,11 +47,13 @@ def tile_decoder_attn_kernel(tc, base, emb, hid, w_ih, w_hh, b_ih, b_hh, offs, o
         nc.sync.dma_start(emb_sb[:], emb)
         hid_sb = held.tile([P, N], BF16, name="hid_sb")
         nc.scalar.dma_start(hid_sb[:], hid)
-        b_ih_sb = held.tile([P, GATES], F32, name="b_ih_sb")
-        b_hh_sb = held.tile([P, GATES], F32, name="b_hh_sb")
-        with nc.allow_non_contiguous_dma(reason="384 bias values, one to a partition and gate"):
-            nc.sync.dma_start(b_ih_sb[:], b_ih.rearrange("(g c) o -> c (g o)", g=GATES))
-            nc.scalar.dma_start(b_hh_sb[:], b_hh.rearrange("(g c) o -> c (g o)", g=GATES))
+        b_rows = held.tile([P, P], F32, name="b_rows", align_bytes=64)
+        nc.gpsimd.memset(b_rows[:], 0.0)
+        for row, queue, b in ((0, nc.sync, b_ih), (1, nc.scalar, b_hh)):
+            queue.dma_start(
+                b_rows[row::BLK, 0 : GATES * BLK].rearrange("q (g j) -> q g j", g=GATES),
+                b.rearrange("(g q j) o -> q g (j o)", g=GATES, j=BLK),
+            )
         offsets = held.tile([P, N // 16], U16, name="offsets")
         nc.sync.dma_start(offsets[:], offs)
         window = held.tile([P, S], F32, name="window")
@@ -67,10 +70,13 @@ def tile_decoder_attn_kernel(tc, base, emb, hid, w_ih, w_hh, b_ih, b_hh, offs, o
         for i in range(WARM_MATMULS):
             nc.tensor.matmul(ps_z[BANKS - 1][:, 0:P], zeros[:], zeros[:], start=True, stop=True)
 
+        b_cols = held.tile([P, P], F32, name="b_cols", align_bytes=64)
+        nc.vector.transpose(b_cols[:], b_rows[:])
         b_sum = held.tile([P, 2], F32, name="b_sum")
-        nc.vector.tensor_tensor(b_sum[:], b_ih_sb[:, 0:2], b_hh_sb[:, 0:2], ADD)
+        nc.vector.tensor_tensor(b_sum[:], b_cols[:, 0 : 2 * BLK : BLK], b_cols[:, 1 : 2 * BLK : BLK], ADD)
         b_in_neg = held.tile([P, 1], F32, name="b_in_neg")
-        nc.vector.tensor_scalar_mul(b_in_neg[:], b_ih_sb[:, 2:3], -1.0)
+        nc.vector.tensor_scalar_mul(b_in_neg[:], b_cols[:, 2 * BLK : 2 * BLK + 1], -1.0)
+        b_hh_n = b_cols[:, 2 * BLK + 1 : 2 * BLK + 2]
 
         ps_r = [psum.tile([P, WB], F32, name=f"ps_r{b}") for b in range(BANKS)]
         ps_gi_n = [psum.tile([P, WB], F32, name=f"ps_gi_n{b}") for b in range(BANKS)]
@@ -95,7 +101,7 @@ def tile_decoder_attn_kernel(tc, base, emb, hid, w_ih, w_hh, b_ih, b_hh, offs, o
         for c in range(CHUNKS):
             nc.scalar.activation(r[:, cols(c)], in_bank(ps_r, c), SIGMOID, bias=b_sum[:, 0:1], scale=1.0)
             nc.vector.scalar_tensor_tensor(
-                r_gh[:, cols(c)], in_bank(ps_gh_n, c), b_hh_sb[:, 2:3], r[:, cols(c)], ADD, MULT
+                r_gh[:, cols(c)], in_bank(ps_gh_n, c), b_hh_n, r[:, cols(c)], ADD, MULT
             )
             nc.vector.tensor_tensor(pre[:, cols(c)], r_gh[:, cols(c)], in_bank(ps_gi_n, c), ADD)
         for b in range(BANKS):

@@ -70,10 +70,14 @@ def tile_decoder_attn_kernel(tc, base, emb, hid, w_ih, w_hh, b_ih, b_hh, offs, o
         for i in range(WARM_MATMULS):
             nc.tensor.matmul(ps_z[BANKS - 1][:, 0:P], zeros[:], zeros[:], start=True, stop=True)
 
+        b_cols_r = held.tile([P, BLK], F32, name="b_cols_r", align_bytes=64)
+        nc.vector.transpose(b_cols_r[:], b_rows[:, 0:BLK])
+        b_sum_r = held.tile([P, 1], F32, name="b_sum_r")
+        nc.vector.tensor_tensor(b_sum_r[:], b_cols_r[:, 0:1], b_cols_r[:, 1:2], ADD)
         b_cols = held.tile([P, P], F32, name="b_cols", align_bytes=64)
         nc.vector.transpose(b_cols[:], b_rows[:])
-        b_sum = held.tile([P, 2], F32, name="b_sum")
-        nc.vector.tensor_tensor(b_sum[:], b_cols[:, 0 : 2 * BLK : BLK], b_cols[:, 1 : 2 * BLK : BLK], ADD)
+        b_sum_z = held.tile([P, 1], F32, name="b_sum_z")
+        nc.vector.tensor_tensor(b_sum_z[:], b_cols[:, BLK : BLK + 1], b_cols[:, BLK + 1 : BLK + 2], ADD)
         b_in_neg = held.tile([P, 1], F32, name="b_in_neg")
         nc.vector.tensor_scalar_mul(b_in_neg[:], b_cols[:, 2 * BLK : 2 * BLK + 1], -1.0)
         b_hh_n = b_cols[:, 2 * BLK + 1 : 2 * BLK + 2]
@@ -99,14 +103,14 @@ def tile_decoder_attn_kernel(tc, base, emb, hid, w_ih, w_hh, b_ih, b_hh, offs, o
         cand_neg = held.tile([P, N], F32, name="cand_neg")
         fresh = held.tile([P, N], F32, name="fresh")
         for c in range(CHUNKS):
-            nc.scalar.activation(r[:, cols(c)], in_bank(ps_r, c), SIGMOID, bias=b_sum[:, 0:1], scale=1.0)
+            nc.scalar.activation(r[:, cols(c)], in_bank(ps_r, c), SIGMOID, bias=b_sum_r[:], scale=1.0)
             nc.vector.scalar_tensor_tensor(
                 r_gh[:, cols(c)], in_bank(ps_gh_n, c), b_hh_n, r[:, cols(c)], ADD, MULT
             )
             nc.vector.tensor_tensor(pre[:, cols(c)], r_gh[:, cols(c)], in_bank(ps_gi_n, c), ADD)
         for b in range(BANKS):
             x = bank_cols(b)
-            nc.scalar.activation(z[:, x], ps_z[b][:], SIGMOID, bias=b_sum[:, 1:2], scale=1.0)
+            nc.scalar.activation(z[:, x], ps_z[b][:], SIGMOID, bias=b_sum_z[:], scale=1.0)
             nc.vector.tensor_tensor(kept[:, x], z[:, x], hid_sb[:, x], MULT)
         for c in range(CHUNKS):
             nc.scalar.activation(cand_neg[:, cols(c)], pre[:, cols(c)], TANH, bias=b_in_neg[:], scale=-1.0)

@@ -49,8 +49,8 @@ def tile_decoder_attn_kernel(tc, base, emb, hid, w_ih, w_hh, b_ih, b_hh, offs, o
         nc.scalar.dma_start(hid_sb[:], hid)
         b_rows = held.tile([P, P], F32, name="b_rows", align_bytes=64)
         nc.gpsimd.memset(b_rows[:], 0.0)
-        for row, queue, b in ((0, nc.sync, b_ih), (1, nc.scalar, b_hh)):
-            queue.dma_start(
+        for row, b in ((0, b_ih), (1, b_hh)):
+            nc.sync.dma_start(
                 b_rows[row::BLK, 0 : GATES * BLK].rearrange("q (g j) -> q g j", g=GATES),
                 b.rearrange("(g q j) o -> q g (j o)", g=GATES, j=BLK),
             )

@@ -47,11 +47,11 @@ def tile_decoder_attn_kernel(tc, base, emb, hid, w_ih, w_hh, b_ih, b_hh, offs, o
         nc.sync.dma_start(emb_sb[:], emb)
         hid_sb = held.tile([P, N], BF16, name="hid_sb")
         nc.scalar.dma_start(hid_sb[:], hid)
-        b_rows = held.tile([P, P], F32, name="b_rows", align_bytes=64)
-        nc.gpsimd.memset(b_rows[:], 0.0)
+        b_rows = held.tile([P, GATES * BLK], F32, name="b_rows", align_bytes=64)
+        nc.vector.memset(b_rows[:], 0.0)
         for row, b in ((0, b_ih), (1, b_hh)):
             nc.sync.dma_start(
-                b_rows[row::BLK, 0 : GATES * BLK].rearrange("q (g j) -> q g j", g=GATES),
+                b_rows[row::BLK, :].rearrange("q (g j) -> q g j", g=GATES),
                 b.rearrange("(g q j) o -> q g (j o)", g=GATES, j=BLK),
             )
         offsets = held.tile([P, N // 16], U16, name="offsets")
@@ -70,17 +70,17 @@ def tile_decoder_attn_kernel(tc, base, emb, hid, w_ih, w_hh, b_ih, b_hh, offs, o
         for i in range(WARM_MATMULS):
             nc.tensor.matmul(ps_z[BANKS - 1][:, 0:P], zeros[:], zeros[:], start=True, stop=True)
 
-        b_cols_r = held.tile([P, BLK], F32, name="b_cols_r", align_bytes=64)
-        nc.vector.transpose(b_cols_r[:], b_rows[:, 0:BLK])
-        b_sum_r = held.tile([P, 1], F32, name="b_sum_r")
-        nc.vector.tensor_tensor(b_sum_r[:], b_cols_r[:, 0:1], b_cols_r[:, 1:2], ADD)
-        b_cols = held.tile([P, P], F32, name="b_cols", align_bytes=64)
-        nc.vector.transpose(b_cols[:], b_rows[:])
-        b_sum_z = held.tile([P, 1], F32, name="b_sum_z")
-        nc.vector.tensor_tensor(b_sum_z[:], b_cols[:, BLK : BLK + 1], b_cols[:, BLK + 1 : BLK + 2], ADD)
+        b_cols = []
+        for g in range(GATES):
+            b_cols.append(held.tile([P, BLK], F32, name=f"b_cols{g}", align_bytes=64))
+            nc.vector.transpose(b_cols[g][:], b_rows[:, g * BLK : (g + 1) * BLK])
+        b_sum = []
+        for g in range(2):
+            b_sum.append(held.tile([P, 1], F32, name=f"b_sum{g}"))
+            nc.vector.tensor_tensor(b_sum[g][:], b_cols[g][:, 0:1], b_cols[g][:, 1:2], ADD)
         b_in_neg = held.tile([P, 1], F32, name="b_in_neg")
-        nc.vector.tensor_scalar_mul(b_in_neg[:], b_cols[:, 2 * BLK : 2 * BLK + 1], -1.0)
-        b_hh_n = b_cols[:, 2 * BLK + 1 : 2 * BLK + 2]
+        nc.vector.tensor_scalar_mul(b_in_neg[:], b_cols[2][:, 0:1], -1.0)
+        b_hh_n = b_cols[2][:, 1:2]
 
         ps_r = [psum.tile([P, WB], F32, name=f"ps_r{b}") for b in range(BANKS)]
         ps_gi_n = [psum.tile([P, WB], F32, name=f"ps_gi_n{b}") for b in range(BANKS)]
@@ -103,14 +103,14 @@ def tile_decoder_attn_kernel(tc, base, emb, hid, w_ih, w_hh, b_ih, b_hh, offs, o
         cand_neg = held.tile([P, N], F32, name="cand_neg")
         fresh = held.tile([P, N], F32, name="fresh")
         for c in range(CHUNKS):
-            nc.scalar.activation(r[:, cols(c)], in_bank(ps_r, c), SIGMOID, bias=b_sum_r[:], scale=1.0)
+            nc.scalar.activation(r[:, cols(c)], in_bank(ps_r, c), SIGMOID, bias=b_sum[0][:], scale=1.0)
             nc.vector.scalar_tensor_tensor(
                 r_gh[:, cols(c)], in_bank(ps_gh_n, c), b_hh_n, r[:, cols(c)], ADD, MULT
             )
             nc.vector.tensor_tensor(pre[:, cols(c)], r_gh[:, cols(c)], in_bank(ps_gi_n, c), ADD)
         for b in range(BANKS):
             x = bank_cols(b)
-            nc.scalar.activation(z[:, x], ps_z[b][:], SIGMOID, bias=b_sum_z[:], scale=1.0)
+            nc.scalar.activation(z[:, x], ps_z[b][:], SIGMOID, bias=b_sum[1][:], scale=1.0)
             nc.vector.tensor_tensor(kept[:, x], z[:, x], hid_sb[:, x], MULT)
         for c in range(CHUNKS):
             nc.scalar.activation(cand_neg[:, cols(c)], pre[:, cols(c)], TANH, bias=b_in_neg[:], scale=-1.0)

@@ -18,6 +18,7 @@ FLOPS = 2 * 2 * P * GATES * P * N
 BF16, F32, U16 = mybir.dt.bfloat16, mybir.dt.float32, mybir.dt.uint16
 ADD, MULT = mybir.AluOpType.add, mybir.AluOpType.mult
 SIGMOID, TANH = mybir.ActivationFunctionType.Sigmoid, mybir.ActivationFunctionType.Tanh
+IDENTITY = mybir.ActivationFunctionType.Identity
 
 
 def cols(c):
@@ -77,7 +78,7 @@ def tile_decoder_attn_kernel(tc, base, emb, hid, w_ih, w_hh, b_ih, b_hh, offs, o
         b_sum = []
         for g in range(2):
             b_sum.append(held.tile([P, 1], F32, name=f"b_sum{g}"))
-            nc.vector.tensor_tensor(b_sum[g][:], b_cols[g][:, 0:1], b_cols[g][:, 1:2], ADD)
+            nc.scalar.activation(b_sum[g][:], b_cols[g][:, 0:1], IDENTITY, bias=b_cols[g][:, 1:2], scale=1.0)
         b_in_neg = held.tile([P, 1], F32, name="b_in_neg")
         nc.vector.tensor_scalar_mul(b_in_neg[:], b_cols[2][:, 0:1], -1.0)
         b_hh_n = b_cols[2][:, 1:2]

import concourse.mybir as mybir

P = 128
N = 512
S = 1024
GATES = 3
BLK = 32
RESET, UPDATE, CAND = slice(0, P), slice(P, 2 * P), slice(2 * P, 3 * P)
BANKS = 2
WB = N // BANKS
CHUNKS = 4
W = N // CHUNKS

WARM_MATMULS = 12

FLOPS = 2 * 2 * P * GATES * P * N

BF16, F32, U16 = mybir.dt.bfloat16, mybir.dt.float32, mybir.dt.uint16
ADD, MULT = mybir.AluOpType.add, mybir.AluOpType.mult
SIGMOID, TANH = mybir.ActivationFunctionType.Sigmoid, mybir.ActivationFunctionType.Tanh
IDENTITY = mybir.ActivationFunctionType.Identity


def cols(c):
    return slice(c * W, (c + 1) * W)


def bank_cols(b):
    return slice(b * WB, (b + 1) * WB)


def in_bank(tiles, c):
    b, start = divmod(c * W, WB)
    return tiles[b][:, start : start + W]


def tile_decoder_attn_kernel(tc, base, emb, hid, w_ih, w_hh, b_ih, b_hh, offs, out):
    nc = tc.nc
    with (
        tc.tile_pool(name="held", bufs=1) as held,
        tc.psum_pool(name="psum", bufs=1) as psum,
    ):
        w_ih_sb = held.tile([P, GATES * P], BF16, name="w_ih_sb")
        nc.sync.dma_start(w_ih_sb[:], w_ih)
        w_hh_sb = held.tile([P, GATES * P], BF16, name="w_hh_sb")
        nc.scalar.dma_start(w_hh_sb[:], w_hh)
        emb_sb = held.tile([P, N], BF16, name="emb_sb")
        nc.sync.dma_start(emb_sb[:], emb)
        hid_sb = held.tile([P, N], BF16, name="hid_sb")
        nc.scalar.dma_start(hid_sb[:], hid)
        b_rows = held.tile([P, GATES * BLK], F32, name="b_rows", align_bytes=64)
        nc.vector.memset(b_rows[:], 0.0)
        for row, b in ((0, b_ih), (1, b_hh)):
            nc.sync.dma_start(
                b_rows[row::BLK, :].rearrange("q (g j) -> q g j", g=GATES),
                b.rearrange("(g q j) o -> q g (j o)", g=GATES, j=BLK),
            )
        offsets = held.tile([P, N // 16], U16, name="offsets")
        nc.sync.dma_start(offsets[:], offs)
        window = held.tile([P, S], F32, name="window")
        nc.gpsimd.dma_start(window[:], base)

        tiny = held.tile([P, 1], F32, name="tiny")
        nc.gpsimd.memset(tiny[:], 0.0)
        tiny_out = held.tile([P, 1], F32, name="tiny_out")
        nc.scalar.activation(tiny_out[:], tiny[:], SIGMOID)

        zeros = held.tile([P, P], BF16, name="zeros")
        nc.vector.memset(zeros[:], 0.0)
        ps_z = [psum.tile([P, WB], F32, name=f"ps_z{b}") for b in range(BANKS)]
        for i in range(WARM_MATMULS):
            nc.tensor.matmul(ps_z[BANKS - 1][:, 0:P], zeros[:], zeros[:], start=True, stop=True)

        b_cols = []
        for g in range(GATES):
            b_cols.append(held.tile([P, BLK], F32, name=f"b_cols{g}", align_bytes=64))
            nc.vector.transpose(b_cols[g][:], b_rows[:, g * BLK : (g + 1) * BLK])
        b_sum = []
        for g in range(2):
            b_sum.append(held.tile([P, 1], F32, name=f"b_sum{g}"))
            nc.scalar.activation(b_sum[g][:], b_cols[g][:, 0:1], IDENTITY, bias=b_cols[g][:, 1:2], scale=1.0)
        b_in_neg = held.tile([P, 1], F32, name="b_in_neg")
        nc.vector.tensor_scalar_mul(b_in_neg[:], b_cols[2][:, 0:1], -1.0)
        b_hh_n = b_cols[2][:, 1:2]

        ps_r = [psum.tile([P, WB], F32, name=f"ps_r{b}") for b in range(BANKS)]
        ps_gi_n = [psum.tile([P, WB], F32, name=f"ps_gi_n{b}") for b in range(BANKS)]
        ps_gh_n = [psum.tile([P, WB], F32, name=f"ps_gh_n{b}") for b in range(BANKS)]
        for b in range(BANKS):
            nc.tensor.matmul(ps_r[b][:], w_ih_sb[:, RESET], emb_sb[:, bank_cols(b)], start=True, stop=False)
            nc.tensor.matmul(ps_r[b][:], w_hh_sb[:, RESET], hid_sb[:, bank_cols(b)], start=False, stop=True)
        for b in range(BANKS):
            nc.tensor.matmul(ps_gh_n[b][:], w_hh_sb[:, CAND], hid_sb[:, bank_cols(b)], start=True, stop=True)
        for b in range(BANKS):
            nc.tensor.matmul(ps_z[b][:], w_ih_sb[:, UPDATE], emb_sb[:, bank_cols(b)], start=True, stop=False)
            nc.tensor.matmul(ps_z[b][:], w_hh_sb[:, UPDATE], hid_sb[:, bank_cols(b)], start=False, stop=True)
            nc.tensor.matmul(ps_gi_n[b][:], w_ih_sb[:, CAND], emb_sb[:, bank_cols(b)], start=True, stop=True)

        r = held.tile([P, N], F32, name="r")
        r_gh = held.tile([P, N], F32, name="r_gh")
        pre = held.tile([P, N], F32, name="pre")
        z = held.tile([P, N], F32, name="z")
        kept = held.tile([P, N], F32, name="kept")
        cand_neg = held.tile([P, N], F32, name="cand_neg")
        fresh = held.tile([P, N], F32, name="fresh")
        for c in range(CHUNKS):
            nc.scalar.activation(r[:, cols(c)], in_bank(ps_r, c), SIGMOID, bias=b_sum[0][:], scale=1.0)
            nc.vector.scalar_tensor_tensor(
                r_gh[:, cols(c)], in_bank(ps_gh_n, c), b_hh_n, r[:, cols(c)], ADD, MULT
            )
            nc.vector.tensor_tensor(pre[:, cols(c)], r_gh[:, cols(c)], in_bank(ps_gi_n, c), ADD)
        for b in range(BANKS):
            x = bank_cols(b)
            nc.scalar.activation(z[:, x], ps_z[b][:], SIGMOID, bias=b_sum[1][:], scale=1.0)
            nc.vector.tensor_tensor(kept[:, x], z[:, x], hid_sb[:, x], MULT)
        for c in range(CHUNKS):
            nc.scalar.activation(cand_neg[:, cols(c)], pre[:, cols(c)], TANH, bias=b_in_neg[:], scale=-1.0)
            nc.vector.scalar_tensor_tensor(
                fresh[:, cols(c)], z[:, cols(c)], -1.0, cand_neg[:, cols(c)], ADD, MULT
            )

        nc.vector.tensor_tensor(window[:].indirect(offsets[:]), fresh[:], kept[:], ADD)
        nc.sync.dma_start(out, window[:])
